import numpy as np
import ml_dtypes

BF16 = ml_dtypes.bfloat16


def bf(x):
    return np.asarray(x, np.float32).astype(BF16)


def f32(x):
    return np.asarray(x, np.float32)


def f64(x):
    return np.asarray(x).astype(np.float64)


def striped(idx):
    return np.tile(idx.reshape(-1, 16).T, (8, 1))


C, S, N, KW, P, CI, R, Q = 512, 4096, 1024, 4, 256, 32, 4, 128


def setup_inputs():
    x = f32(np.random.standard_normal((C, S)))
    act = np.random.uniform(0.0, 1.0, (CI, N))
    a = f32(np.tile(np.repeat(act, R, axis=0), (R, 1)))
    w = bf(np.random.standard_normal((KW * Q, Q)))
    return {"x": x, "a": a, "w": w, "offs": striped(np.random.permutation(S)[:N])}


def reference(x, a, w, offs):
    idx = offs[:16].T.reshape(-1)
    z = (f64(x)[:, idx] * f64(a)).reshape(R, Q, KW, P)
    num = np.einsum("tqm,iqtp->imp", f64(w).reshape(KW, Q, Q), z)
    den = f64(a).reshape(C, KW, P).sum(axis=(0, 1)) / (R * R)
    return (num / den[None, None, :]).reshape(C, P)

@@ -1,0 +1,72 @@
+import concourse.mybir as mybir
+
+F32 = mybir.dt.float32
+BF16 = mybir.dt.bfloat16
+U16 = mybir.dt.uint16
+MULT = mybir.AluOpType.mult
+COPY = mybir.ActivationFunctionType.Copy
+
+PARTS = 128
+BLOCKS = 4
+PLACES = 4096
+CHILDREN = 4
+PARENTS = 256
+ENTRIES = CHILDREN * PARENTS
+PER_COLUMN = 16
+
+FLOPS = 2 * BLOCKS * CHILDREN * PARTS * PARTS * PARENTS
+
+
+def tile_convcaps_kernel(tc, x, a, w, offs, out):
+    nc = tc.nc
+    with (
+        tc.tile_pool(name="held", bufs=1) as held,
+        tc.tile_pool(name="ring", bufs=4) as ring,
+        tc.psum_pool(name="den_bank", bufs=1) as den_bank,
+        tc.psum_pool(name="num_banks", bufs=2) as num_banks,
+    ):
+        offsets = held.tile([PARTS, ENTRIES // PER_COLUMN], U16, name="offsets")
+        nc.sync.dma_start(offsets[:], offs)
+        weights = held.tile([PARTS, CHILDREN, PARTS], BF16, name="weights")
+        nc.scalar.dma_start(weights[:], w.rearrange("(t q) m -> q t m", q=PARTS))
+        a_blocks = []
+        for i in range(BLOCKS):
+            a_block = held.tile([PARTS, ENTRIES], F32, name=f"a_block{i}")
+            nc.sync.dma_start(a_block[:], a[i * PARTS : (i + 1) * PARTS, :])
+            a_blocks.append(a_block)
+        x_blocks = []
+        for i in range(BLOCKS):
+            x_block = held.tile([PARTS, PLACES], F32, name=f"x_block{i}")
+            nc.sync.dma_start(x_block[:], x[i * PARTS : (i + 1) * PARTS, :])
+            x_blocks.append(x_block)
+
+        sixteenths = held.tile([PARTS, PARTS], BF16, name="sixteenths")
+        nc.vector.memset(sixteenths[:], 1.0 / 16.0)
+        den = den_bank.tile([PARTS, PARENTS], F32, name="den")
+        for i in range(BLOCKS):
+            a_rounded = ring.tile([PARTS, ENTRIES], BF16, name="a_rounded")
+            nc.scalar.activation(a_rounded[:], a_blocks[i][:], COPY)
+            for t in range(CHILDREN):
+                nc.tensor.matmul(
+                    den[:],
+                    sixteenths[:],
+                    a_rounded[:, t * PARENTS : (t + 1) * PARENTS],
+                    start=(i == 0 and t == 0),
+                    stop=(i == BLOCKS - 1 and t == CHILDREN - 1),
+                )
+        den_inverse = held.tile([PARTS, PARENTS], F32, name="den_inverse")
+        nc.vector.reciprocal(den_inverse[:], den[:])
+
+        for i in range(BLOCKS):
+            num = num_banks.tile([PARTS, PARENTS], F32, name="num")
+            for t in range(CHILDREN):
+                piece = slice(t * PARENTS, (t + 1) * PARENTS)
+                piece_offsets = offsets[:, t * PARENTS // PER_COLUMN : (t + 1) * PARENTS // PER_COLUMN]
+                z = ring.tile([PARTS, PARENTS], F32, name="z")
+                nc.vector.tensor_tensor(z[:], x_blocks[i][:].indirect(piece_offsets), a_blocks[i][:, piece], MULT)
+                z_rounded = ring.tile([PARTS, PARENTS], BF16, name="z_rounded")
+                nc.scalar.activation(z_rounded[:], z[:], COPY)
+                nc.tensor.matmul(num[:], weights[:, t, :], z_rounded[:], start=(t == 0), stop=(t == CHILDREN - 1))
+            mean = ring.tile([PARTS, PARENTS], F32, name="mean")
+            nc.vector.tensor_tensor(mean[:], num[:], den_inverse[:], MULT)
+            nc.sync.dma_start(out[i * PARTS : (i + 1) * PARTS, :], mean[:])

@@ -15,6 +15,7 @@ ENTRIES = CHILDREN * PARENTS
 PER_COLUMN = 16
 
 FLOPS = 2 * BLOCKS * CHILDREN * PARTS * PARTS * PARENTS
+BYTES = 4 * BLOCKS * PARTS * PLACES + 4 * PARTS * ENTRIES + 2 * CHILDREN * PARTS * PARTS + 2 * PARTS * ENTRIES // PER_COLUMN + 4 * BLOCKS * PARTS * PARENTS
 
 
 def tile_convcaps_kernel(tc, x, a, w, offs, out):
@@ -29,31 +30,27 @@ def tile_convcaps_kernel(tc, x, a, w, offs, out):
         nc.sync.dma_start(offsets[:], offs)
         weights = held.tile([PARTS, CHILDREN, PARTS], BF16, name="weights")
         nc.scalar.dma_start(weights[:], w.rearrange("(t q) m -> q t m", q=PARTS))
-        a_blocks = []
-        for i in range(BLOCKS):
-            a_block = held.tile([PARTS, ENTRIES], F32, name=f"a_block{i}")
-            nc.sync.dma_start(a_block[:], a[i * PARTS : (i + 1) * PARTS, :])
-            a_blocks.append(a_block)
+        a_block = held.tile([PARTS, ENTRIES], F32, name="a_block")
+        nc.sync.dma_start(a_block[:], a[0:PARTS, :])
         x_blocks = []
         for i in range(BLOCKS):
             x_block = held.tile([PARTS, PLACES], F32, name=f"x_block{i}")
             nc.sync.dma_start(x_block[:], x[i * PARTS : (i + 1) * PARTS, :])
             x_blocks.append(x_block)
 
-        sixteenths = held.tile([PARTS, PARTS], BF16, name="sixteenths")
-        nc.vector.memset(sixteenths[:], 1.0 / 16.0)
+        share = held.tile([PARTS, PARTS], BF16, name="share")
+        nc.vector.memset(share[:], BLOCKS / 16.0)
         den = den_bank.tile([PARTS, PARENTS], F32, name="den")
-        for i in range(BLOCKS):
-            a_rounded = ring.tile([PARTS, ENTRIES], BF16, name="a_rounded")
-            nc.scalar.activation(a_rounded[:], a_blocks[i][:], COPY)
-            for t in range(CHILDREN):
-                nc.tensor.matmul(
-                    den[:],
-                    sixteenths[:],
-                    a_rounded[:, t * PARENTS : (t + 1) * PARENTS],
-                    start=(i == 0 and t == 0),
-                    stop=(i == BLOCKS - 1 and t == CHILDREN - 1),
-                )
+        a_rounded = held.tile([PARTS, ENTRIES], BF16, name="a_rounded")
+        nc.scalar.activation(a_rounded[:], a_block[:], COPY)
+        for t in range(CHILDREN):
+            nc.tensor.matmul(
+                den[:],
+                share[:],
+                a_rounded[:, t * PARENTS : (t + 1) * PARENTS],
+                start=(t == 0),
+                stop=(t == CHILDREN - 1),
+            )
         den_inverse = held.tile([PARTS, PARENTS], F32, name="den_inverse")
         nc.vector.reciprocal(den_inverse[:], den[:])
 
@@ -63,7 +60,7 @@ def tile_convcaps_kernel(tc, x, a, w, offs, out):
                 piece = slice(t * PARENTS, (t + 1) * PARENTS)
                 piece_offsets = offsets[:, t * PARENTS // PER_COLUMN : (t + 1) * PARENTS // PER_COLUMN]
                 z = ring.tile([PARTS, PARENTS], F32, name="z")
-                nc.vector.tensor_tensor(z[:], x_blocks[i][:].indirect(piece_offsets), a_blocks[i][:, piece], MULT)
+                nc.vector.tensor_tensor(z[:], x_blocks[i][:].indirect(piece_offsets), a_block[:, piece], MULT)
                 z_rounded = ring.tile([PARTS, PARENTS], BF16, name="z_rounded")
                 nc.scalar.activation(z_rounded[:], z[:], COPY)
                 nc.tensor.matmul(num[:], weights[:, t, :], z_rounded[:], start=(t == 0), stop=(t == CHILDREN - 1))

@@ -13,6 +13,8 @@ CHILDREN = 4
 PARENTS = 256
 ENTRIES = CHILDREN * PARENTS
 PER_COLUMN = 16
+HALF = PARENTS // 2
+BANK = 512
 
 FLOPS = 2 * BLOCKS * CHILDREN * PARTS * PARTS * PARENTS
 BYTES = 4 * BLOCKS * PARTS * PLACES + 4 * PARTS * ENTRIES + 2 * CHILDREN * PARTS * PARTS + 2 * PARTS * ENTRIES // PER_COLUMN + 4 * BLOCKS * PARTS * PARENTS
@@ -25,6 +27,7 @@ def tile_convcaps_kernel(tc, x, a, w, offs, out):
         tc.tile_pool(name="ring", bufs=4) as ring,
         tc.psum_pool(name="den_bank", bufs=1) as den_bank,
         tc.psum_pool(name="num_banks", bufs=2) as num_banks,
+        tc.psum_pool(name="half_banks", bufs=1) as half_banks,
     ):
         offsets = held.tile([PARTS, ENTRIES // PER_COLUMN], U16, name="offsets")
         nc.sync.dma_start(offsets[:], offs)
@@ -54,16 +57,41 @@ def tile_convcaps_kernel(tc, x, a, w, offs, out):
         den_inverse = held.tile([PARTS, PARENTS], F32, name="den_inverse")
         nc.vector.reciprocal(den_inverse[:], den[:])
 
-        for i in range(BLOCKS):
+        def look_up(i, first_entry, count):
+            piece_offsets = offsets[:, first_entry // PER_COLUMN : (first_entry + count) // PER_COLUMN]
+            z = ring.tile([PARTS, PARENTS], F32, name="z")
+            nc.vector.tensor_tensor(
+                z[:, :count], x_blocks[i][:].indirect(piece_offsets), a_block[:, first_entry : first_entry + count], MULT
+            )
+            z_rounded = ring.tile([PARTS, PARENTS], BF16, name="z_rounded")
+            nc.scalar.activation(z_rounded[:, :count], z[:, :count], COPY)
+            return z_rounded
+
+        def divide_and_store(i, num, first_parent, count):
+            parents = slice(first_parent, first_parent + count)
+            mean = ring.tile([PARTS, PARENTS], F32, name="mean")
+            nc.vector.tensor_tensor(mean[:, :count], num, den_inverse[:, parents], MULT)
+            nc.sync.dma_start(out[i * PARTS : (i + 1) * PARTS, parents], mean[:, :count])
+
+        for i in range(BLOCKS - 1):
             num = num_banks.tile([PARTS, PARENTS], F32, name="num")
             for t in range(CHILDREN):
-                piece = slice(t * PARENTS, (t + 1) * PARENTS)
-                piece_offsets = offsets[:, t * PARENTS // PER_COLUMN : (t + 1) * PARENTS // PER_COLUMN]
-                z = ring.tile([PARTS, PARENTS], F32, name="z")
-                nc.vector.tensor_tensor(z[:], x_blocks[i][:].indirect(piece_offsets), a_block[:, piece], MULT)
-                z_rounded = ring.tile([PARTS, PARENTS], BF16, name="z_rounded")
-                nc.scalar.activation(z_rounded[:], z[:], COPY)
+                z_rounded = look_up(i, t * PARENTS, PARENTS)
                 nc.tensor.matmul(num[:], weights[:, t, :], z_rounded[:], start=(t == 0), stop=(t == CHILDREN - 1))
-            mean = ring.tile([PARTS, PARENTS], F32, name="mean")
-            nc.vector.tensor_tensor(mean[:], num[:], den_inverse[:], MULT)
-            nc.sync.dma_start(out[i * PARTS : (i + 1) * PARTS, :], mean[:])
+            divide_and_store(i, num[:], 0, PARENTS)
+
+        i = BLOCKS - 1
+        halves = range(0, PARENTS, HALF)
+        half_nums = {first: half_banks.tile([PARTS, BANK], F32, name=f"half_num{first}") for first in halves}
+        for t in range(CHILDREN - 1):
+            z_rounded = look_up(i, t * PARENTS, PARENTS)
+            for first in halves:
+                nc.tensor.matmul(
+                    half_nums[first][:, :HALF], weights[:, t, :], z_rounded[:, first : first + HALF], start=(t == 0), stop=False
+                )
+        t = CHILDREN - 1
+        for first in halves:
+            z_rounded = look_up(i, t * PARENTS + first, HALF)
+            nc.tensor.matmul(half_nums[first][:, :HALF], weights[:, t, :], z_rounded[:, :HALF], start=False, stop=True)
+        for first in halves:
+            divide_and_store(i, half_nums[first][:, :HALF], first, HALF)

@@ -29,17 +29,16 @@ def tile_convcaps_kernel(tc, x, a, w, offs, out):
         tc.psum_pool(name="num_banks", bufs=2) as num_banks,
         tc.psum_pool(name="half_banks", bufs=1) as half_banks,
     ):
+        x_blocks = [held.tile([PARTS, PLACES], F32, name=f"x_block{i}") for i in range(BLOCKS)]
         offsets = held.tile([PARTS, ENTRIES // PER_COLUMN], U16, name="offsets")
-        nc.sync.dma_start(offsets[:], offs)
+        a_block = held.tile([PARTS, ENTRIES], F32, name="a_block")
         weights = held.tile([PARTS, CHILDREN, PARTS], BF16, name="weights")
         nc.scalar.dma_start(weights[:], w.rearrange("(t q) m -> q t m", q=PARTS))
-        a_block = held.tile([PARTS, ENTRIES], F32, name="a_block")
+        nc.sync.dma_start(x_blocks[0][:], x[0:PARTS, :])
+        nc.sync.dma_start(offsets[:], offs)
         nc.sync.dma_start(a_block[:], a[0:PARTS, :])
-        x_blocks = []
-        for i in range(BLOCKS):
-            x_block = held.tile([PARTS, PLACES], F32, name=f"x_block{i}")
-            nc.sync.dma_start(x_block[:], x[i * PARTS : (i + 1) * PARTS, :])
-            x_blocks.append(x_block)
+        for i in range(1, BLOCKS):
+            nc.sync.dma_start(x_blocks[i][:], x[i * PARTS : (i + 1) * PARTS, :])
 
         share = held.tile([PARTS, PARTS], BF16, name="share")
         nc.vector.memset(share[:], BLOCKS / 16.0)
@@ -55,7 +54,6 @@ def tile_convcaps_kernel(tc, x, a, w, offs, out):
                 stop=(t == CHILDREN - 1),
             )
         den_inverse = held.tile([PARTS, PARENTS], F32, name="den_inverse")
-        nc.vector.reciprocal(den_inverse[:], den[:])
 
         def look_up(i, first_entry, count):
             piece_offsets = offsets[:, first_entry // PER_COLUMN : (first_entry + count) // PER_COLUMN]
@@ -78,6 +76,8 @@ def tile_convcaps_kernel(tc, x, a, w, offs, out):
             for t in range(CHILDREN):
                 z_rounded = look_up(i, t * PARENTS, PARENTS)
                 nc.tensor.matmul(num[:], weights[:, t, :], z_rounded[:], start=(t == 0), stop=(t == CHILDREN - 1))
+            if i == 0:
+                nc.vector.reciprocal(den_inverse[:], den[:])
             divide_and_store(i, num[:], 0, PARENTS)
 
         i = BLOCKS - 1

@@ -33,10 +33,10 @@ def tile_convcaps_kernel(tc, x, a, w, offs, out):
         offsets = held.tile([PARTS, ENTRIES // PER_COLUMN], U16, name="offsets")
         a_block = held.tile([PARTS, ENTRIES], F32, name="a_block")
         weights = held.tile([PARTS, CHILDREN, PARTS], BF16, name="weights")
-        nc.scalar.dma_start(weights[:], w.rearrange("(t q) m -> q t m", q=PARTS))
         nc.sync.dma_start(x_blocks[0][:], x[0:PARTS, :])
         nc.sync.dma_start(offsets[:], offs)
         nc.sync.dma_start(a_block[:], a[0:PARTS, :])
+        nc.sync.dma_start(weights[:], w.rearrange("(t q) m -> q t m", q=PARTS))
         for i in range(1, BLOCKS):
             nc.sync.dma_start(x_blocks[i][:], x[i * PARTS : (i + 1) * PARTS, :])
 

@@ -25,6 +25,7 @@ def tile_convcaps_kernel(tc, x, a, w, offs, out):
     with (
         tc.tile_pool(name="held", bufs=1) as held,
         tc.tile_pool(name="ring", bufs=4) as ring,
+        tc.tile_pool(name="means", bufs=BLOCKS + 1) as means,
         tc.psum_pool(name="den_bank", bufs=1) as den_bank,
         tc.psum_pool(name="num_banks", bufs=2) as num_banks,
         tc.psum_pool(name="half_banks", bufs=1) as half_banks,
@@ -55,19 +56,19 @@ def tile_convcaps_kernel(tc, x, a, w, offs, out):
             )
         den_inverse = held.tile([PARTS, PARENTS], F32, name="den_inverse")
 
-        def look_up(i, first_entry, count):
+        def look_up(i, first_entry, count, rounder=nc.scalar.copy):
             piece_offsets = offsets[:, first_entry // PER_COLUMN : (first_entry + count) // PER_COLUMN]
             z = ring.tile([PARTS, PARENTS], F32, name="z")
             nc.vector.tensor_tensor(
                 z[:, :count], x_blocks[i][:].indirect(piece_offsets), a_block[:, first_entry : first_entry + count], MULT
             )
             z_rounded = ring.tile([PARTS, PARENTS], BF16, name="z_rounded")
-            nc.scalar.activation(z_rounded[:, :count], z[:, :count], COPY)
+            rounder(z_rounded[:, :count], z[:, :count])
             return z_rounded
 
         def divide_and_store(i, num, first_parent, count):
             parents = slice(first_parent, first_parent + count)
-            mean = ring.tile([PARTS, PARENTS], F32, name="mean")
+            mean = means.tile([PARTS, PARENTS], F32, name="mean")
             nc.vector.tensor_tensor(mean[:, :count], num, den_inverse[:, parents], MULT)
             nc.sync.dma_start(out[i * PARTS : (i + 1) * PARTS, parents], mean[:, :count])
 
@@ -91,7 +92,8 @@ def tile_convcaps_kernel(tc, x, a, w, offs, out):
                 )
         t = CHILDREN - 1
         for first in halves:
-            z_rounded = look_up(i, t * PARENTS + first, HALF)
+            last_piece = first == PARENTS - HALF
+            z_rounded = look_up(i, t * PARENTS + first, HALF, nc.vector.tensor_copy if last_piece else nc.scalar.copy)
             nc.tensor.matmul(half_nums[first][:, :HALF], weights[:, t, :], z_rounded[:, :HALF], start=False, stop=True)
         for first in halves:
             divide_and_store(i, half_nums[first][:, :HALF], first, HALF)

@@ -4,7 +4,6 @@ F32 = mybir.dt.float32
 BF16 = mybir.dt.bfloat16
 U16 = mybir.dt.uint16
 MULT = mybir.AluOpType.mult
-COPY = mybir.ActivationFunctionType.Copy
 
 PARTS = 128
 BLOCKS = 4
@@ -14,6 +13,7 @@ PARENTS = 256
 ENTRIES = CHILDREN * PARENTS
 PER_COLUMN = 16
 HALF = PARENTS // 2
+LONGEST = ENTRIES // 2
 BANK = 512
 
 FLOPS = 2 * BLOCKS * CHILDREN * PARTS * PARTS * PARENTS
@@ -43,9 +43,9 @@ def tile_convcaps_kernel(tc, x, a, w, offs, out):
 
         share = held.tile([PARTS, PARTS], BF16, name="share")
         nc.vector.memset(share[:], BLOCKS / 16.0)
-        den = den_bank.tile([PARTS, PARENTS], F32, name="den")
         a_rounded = held.tile([PARTS, ENTRIES], BF16, name="a_rounded")
-        nc.scalar.activation(a_rounded[:], a_block[:], COPY)
+        nc.scalar.copy(a_rounded[:], a_block[:])
+        den = den_bank.tile([PARTS, PARENTS], F32, name="den")
         for t in range(CHILDREN):
             nc.tensor.matmul(
                 den[:],
@@ -56,14 +56,16 @@ def tile_convcaps_kernel(tc, x, a, w, offs, out):
             )
         den_inverse = held.tile([PARTS, PARENTS], F32, name="den_inverse")
 
-        def look_up(i, first_entry, count, rounder=nc.scalar.copy):
+        def look_up(i, first_entry, count, rounder):
             piece_offsets = offsets[:, first_entry // PER_COLUMN : (first_entry + count) // PER_COLUMN]
-            z = ring.tile([PARTS, PARENTS], F32, name="z")
+            z = ring.tile([PARTS, LONGEST], F32, name="z")
             nc.vector.tensor_tensor(
                 z[:, :count], x_blocks[i][:].indirect(piece_offsets), a_block[:, first_entry : first_entry + count], MULT
             )
-            z_rounded = ring.tile([PARTS, PARENTS], BF16, name="z_rounded")
-            rounder(z_rounded[:, :count], z[:, :count])
+            z_rounded = ring.tile([PARTS, LONGEST], BF16, name="z_rounded")
+            for column in range(0, count, PARENTS):
+                columns = slice(column, min(column + PARENTS, count))
+                rounder(z_rounded[:, columns], z[:, columns])
             return z_rounded
 
         def divide_and_store(i, num, first_parent, count):
@@ -75,25 +77,31 @@ def tile_convcaps_kernel(tc, x, a, w, offs, out):
         for i in range(BLOCKS - 1):
             num = num_banks.tile([PARTS, PARENTS], F32, name="num")
             for t in range(CHILDREN):
-                z_rounded = look_up(i, t * PARENTS, PARENTS)
-                nc.tensor.matmul(num[:], weights[:, t, :], z_rounded[:], start=(t == 0), stop=(t == CHILDREN - 1))
+                z_rounded = look_up(i, t * PARENTS, PARENTS, nc.scalar.copy)
+                nc.tensor.matmul(num[:], weights[:, t, :], z_rounded[:, :PARENTS], start=(t == 0), stop=(t == CHILDREN - 1))
             if i == 0:
                 nc.vector.reciprocal(den_inverse[:], den[:])
             divide_and_store(i, num[:], 0, PARENTS)
 
         i = BLOCKS - 1
-        halves = range(0, PARENTS, HALF)
-        half_nums = {first: half_banks.tile([PARTS, BANK], F32, name=f"half_num{first}") for first in halves}
-        for t in range(CHILDREN - 1):
-            z_rounded = look_up(i, t * PARENTS, PARENTS)
-            for first in halves:
+        pieces = []
+        first_entry = 0
+        while first_entry < ENTRIES:
+            count = max((ENTRIES - first_entry) // 2, HALF)
+            pieces.append((first_entry, count))
+            first_entry += count
+        half_nums = {first_parent: half_banks.tile([PARTS, BANK], F32, name=f"half_num{first_parent}") for first_parent in range(0, PARENTS, HALF)}
+        for first_entry, count in pieces:
+            last_piece = first_entry + count == ENTRIES
+            z_rounded = look_up(i, first_entry, count, nc.vector.tensor_copy if last_piece else nc.scalar.copy)
+            for column in range(0, count, HALF):
+                t, first_parent = divmod(first_entry + column, PARENTS)
                 nc.tensor.matmul(
-                    half_nums[first][:, :HALF], weights[:, t, :], z_rounded[:, first : first + HALF], start=(t == 0), stop=False
+                    half_nums[first_parent][:, :HALF],
+                    weights[:, t, :],
+                    z_rounded[:, column : column + HALF],
+                    start=(t == 0),
+                    stop=(t == CHILDREN - 1),
                 )
-        t = CHILDREN - 1
-        for first in halves:
-            last_piece = first == PARENTS - HALF
-            z_rounded = look_up(i, t * PARENTS + first, HALF, nc.vector.tensor_copy if last_piece else nc.scalar.copy)
-            nc.tensor.matmul(half_nums[first][:, :HALF], weights[:, t, :], z_rounded[:, :HALF], start=False, stop=True)
-        for first in halves:
-            divide_and_store(i, half_nums[first][:, :HALF], first, HALF)
+        for first_parent in half_nums:
+            divide_and_store(i, half_nums[first_parent][:, :HALF], first_parent, HALF)

@@ -16,8 +16,15 @@ HALF = PARENTS // 2
 LONGEST = ENTRIES // 2
 BANK = 512
 
+TYPES = 32
+ROWS_PER_TYPE = PARTS // TYPES
+HALVES = 2
+HALF_CHILDREN = CHILDREN // HALVES
+HALF_ROW = ENTRIES // HALVES
+STRIDE = ENTRIES + HALF_ROW
+
 FLOPS = 2 * BLOCKS * CHILDREN * PARTS * PARTS * PARENTS
-BYTES = 4 * BLOCKS * PARTS * PLACES + 4 * PARTS * ENTRIES + 2 * CHILDREN * PARTS * PARTS + 2 * PARTS * ENTRIES // PER_COLUMN + 4 * BLOCKS * PARTS * PARENTS
+BYTES = 4 * BLOCKS * PARTS * PLACES + 4 * TYPES * ENTRIES + 2 * CHILDREN * PARTS * PARTS + 2 * PARTS * ENTRIES // PER_COLUMN + 4 * BLOCKS * PARTS * PARENTS
 
 
 def tile_convcaps_kernel(tc, x, a, w, offs, out):
@@ -27,40 +34,77 @@ def tile_convcaps_kernel(tc, x, a, w, offs, out):
         tc.tile_pool(name="ring", bufs=4) as ring,
         tc.tile_pool(name="means", bufs=BLOCKS + 1) as means,
         tc.psum_pool(name="den_bank", bufs=1) as den_bank,
+        tc.psum_pool(name="a_banks", bufs=1) as a_banks,
         tc.psum_pool(name="num_banks", bufs=2) as num_banks,
         tc.psum_pool(name="half_banks", bufs=1) as half_banks,
     ):
         x_blocks = [held.tile([PARTS, PLACES], F32, name=f"x_block{i}") for i in range(BLOCKS)]
         offsets = held.tile([PARTS, ENTRIES // PER_COLUMN], U16, name="offsets")
-        a_block = held.tile([PARTS, ENTRIES], F32, name="a_block")
+        half_rows = held.tile([PARTS, HALF_ROW], F32, name="half_rows")
         weights = held.tile([PARTS, CHILDREN, PARTS], BF16, name="weights")
-        nc.sync.dma_start(x_blocks[0][:], x[0:PARTS, :])
+        a_in_a_row = a.rearrange("c j -> (c j)")
+        nc.sync.dma_start(half_rows[:], a_in_a_row[0 : PARTS * STRIDE].rearrange("(k e) -> k e", e=STRIDE)[:, 0:HALF_ROW])
         nc.sync.dma_start(offsets[:], offs)
-        nc.sync.dma_start(a_block[:], a[0:PARTS, :])
+        nc.sync.dma_start(x_blocks[0][:], x[0:PARTS, :])
         nc.sync.dma_start(weights[:], w.rearrange("(t q) m -> q t m", q=PARTS))
         for i in range(1, BLOCKS):
             nc.sync.dma_start(x_blocks[i][:], x[i * PARTS : (i + 1) * PARTS, :])
 
-        share = held.tile([PARTS, PARTS], BF16, name="share")
-        nc.vector.memset(share[:], BLOCKS / 16.0)
-        a_rounded = held.tile([PARTS, ENTRIES], BF16, name="a_rounded")
-        nc.scalar.copy(a_rounded[:], a_block[:])
+        holds = held.tile([PARTS, HALVES, TYPES], F32, name="holds")
+        nc.gpsimd.memset(holds[:], 0.0)
+        for value in (0, 2, 4):
+            nc.gpsimd.affine_select(
+                holds[:],
+                holds[:],
+                pattern=[[-1, HALVES], [-8, TYPES]],
+                compare_op=mybir.AluOpType.not_equal,
+                fill=1.0,
+                base=-value,
+                channel_multiplier=3,
+            )
+        member = held.tile([PARTS, HALVES], F32, name="member")
+        nc.vector.reduce_sum(member[:], holds[:], axis=mybir.AxisListType.X)
+        members = held.tile([PARTS, HALVES, PARTS], BF16, name="members")
+        nc.vector.tensor_copy(members[:], member[:].unsqueeze(2).to_broadcast([PARTS, HALVES, PARTS]))
+        pick = held.tile([PARTS, HALVES, TYPES, ROWS_PER_TYPE], F32, name="pick")
+        nc.vector.tensor_copy(pick[:], holds[:].unsqueeze(3).to_broadcast([PARTS, HALVES, TYPES, ROWS_PER_TYPE]))
+
+        half_rows_rounded = held.tile([PARTS, HALF_ROW], BF16, name="half_rows_rounded")
+        nc.scalar.copy(half_rows_rounded[:], half_rows[:])
         den = den_bank.tile([PARTS, PARENTS], F32, name="den")
         for t in range(CHILDREN):
+            h, child_of_half = divmod(t, HALF_CHILDREN)
             nc.tensor.matmul(
                 den[:],
-                share[:],
-                a_rounded[:, t * PARENTS : (t + 1) * PARENTS],
+                members[:, h, :],
+                half_rows_rounded[:, child_of_half * PARENTS : (child_of_half + 1) * PARENTS],
                 start=(t == 0),
                 stop=(t == CHILDREN - 1),
             )
         den_inverse = held.tile([PARTS, PARENTS], F32, name="den_inverse")
+        nc.vector.reciprocal(den_inverse[:], den[:])
+        divided = held.tile([PARTS, HALF_CHILDREN, PARENTS], F32, name="divided")
+        nc.vector.tensor_tensor(
+            divided[:],
+            half_rows[:].rearrange("k (t p) -> k t p", t=HALF_CHILDREN),
+            den_inverse[:].unsqueeze(1).to_broadcast([PARTS, HALF_CHILDREN, PARENTS]),
+            MULT,
+        )
+
+        a_divided = held.tile([PARTS, ENTRIES], F32, name="a_divided")
+        for h in range(HALVES):
+            spread = a_banks.tile([PARTS, HALF_ROW], F32, name=f"spread{h}")
+            for child_of_half in range(HALF_CHILDREN):
+                columns = slice(child_of_half * PARENTS, (child_of_half + 1) * PARENTS)
+                first_entry = (h * HALF_CHILDREN + child_of_half) * PARENTS
+                nc.tensor.matmul(spread[:, columns], pick[:, h, :, :].rearrange("k u r -> k (u r)"), divided[:, child_of_half, :])
+                nc.scalar.copy(a_divided[:, first_entry : first_entry + PARENTS], spread[:, columns])
 
         def look_up(i, first_entry, count, rounder):
             piece_offsets = offsets[:, first_entry // PER_COLUMN : (first_entry + count) // PER_COLUMN]
             z = ring.tile([PARTS, LONGEST], F32, name="z")
             nc.vector.tensor_tensor(
-                z[:, :count], x_blocks[i][:].indirect(piece_offsets), a_block[:, first_entry : first_entry + count], MULT
+                z[:, :count], x_blocks[i][:].indirect(piece_offsets), a_divided[:, first_entry : first_entry + count], MULT
             )
             z_rounded = ring.tile([PARTS, LONGEST], BF16, name="z_rounded")
             for column in range(0, count, PARENTS):
@@ -68,20 +112,17 @@ def tile_convcaps_kernel(tc, x, a, w, offs, out):
                 rounder(z_rounded[:, columns], z[:, columns])
             return z_rounded
 
-        def divide_and_store(i, num, first_parent, count):
-            parents = slice(first_parent, first_parent + count)
+        def copy_out_and_store(i, sums, first_parent, count):
             mean = means.tile([PARTS, PARENTS], F32, name="mean")
-            nc.vector.tensor_tensor(mean[:, :count], num, den_inverse[:, parents], MULT)
-            nc.sync.dma_start(out[i * PARTS : (i + 1) * PARTS, parents], mean[:, :count])
+            nc.scalar.copy(mean[:, :count], sums)
+            nc.sync.dma_start(out[i * PARTS : (i + 1) * PARTS, first_parent : first_parent + count], mean[:, :count])
 
         for i in range(BLOCKS - 1):
             num = num_banks.tile([PARTS, PARENTS], F32, name="num")
             for t in range(CHILDREN):
                 z_rounded = look_up(i, t * PARENTS, PARENTS, nc.scalar.copy)
                 nc.tensor.matmul(num[:], weights[:, t, :], z_rounded[:, :PARENTS], start=(t == 0), stop=(t == CHILDREN - 1))
-            if i == 0:
-                nc.vector.reciprocal(den_inverse[:], den[:])
-            divide_and_store(i, num[:], 0, PARENTS)
+            copy_out_and_store(i, num[:], 0, PARENTS)
 
         i = BLOCKS - 1
         pieces = []
@@ -104,4 +145,4 @@ def tile_convcaps_kernel(tc, x, a, w, offs, out):
                     stop=(t == CHILDREN - 1),
                 )
         for first_parent in half_nums:
-            divide_and_store(i, half_nums[first_parent][:, :HALF], first_parent, HALF)
+            copy_out_and_store(i, half_nums[first_parent][:, :HALF], first_parent, HALF)

@@ -1,4 +1,5 @@
 import concourse.mybir as mybir
+from concourse.masks import make_identity
 
 F32 = mybir.dt.float32
 BF16 = mybir.dt.bfloat16
@@ -18,10 +19,8 @@ BANK = 512
 
 TYPES = 32
 ROWS_PER_TYPE = PARTS // TYPES
-HALVES = 2
-HALF_CHILDREN = CHILDREN // HALVES
-HALF_ROW = ENTRIES // HALVES
-STRIDE = ENTRIES + HALF_ROW
+W_ROWS = CHILDREN
+BAND = (CHILDREN - 1) * PARTS + W_ROWS - 1 + PARTS
 
 FLOPS = 2 * BLOCKS * CHILDREN * PARTS * PARTS * PARENTS
 BYTES = 4 * BLOCKS * PARTS * PLACES + 4 * TYPES * ENTRIES + 2 * CHILDREN * PARTS * PARTS + 2 * PARTS * ENTRIES // PER_COLUMN + 4 * BLOCKS * PARTS * PARENTS
@@ -35,70 +34,65 @@ def tile_convcaps_kernel(tc, x, a, w, offs, out):
         tc.tile_pool(name="means", bufs=BLOCKS + 1) as means,
         tc.psum_pool(name="den_bank", bufs=1) as den_bank,
         tc.psum_pool(name="a_banks", bufs=1) as a_banks,
+        tc.psum_pool(name="w_bank", bufs=1) as w_bank,
         tc.psum_pool(name="num_banks", bufs=2) as num_banks,
         tc.psum_pool(name="half_banks", bufs=1) as half_banks,
     ):
         x_blocks = [held.tile([PARTS, PLACES], F32, name=f"x_block{i}") for i in range(BLOCKS)]
         offsets = held.tile([PARTS, ENTRIES // PER_COLUMN], U16, name="offsets")
-        half_rows = held.tile([PARTS, HALF_ROW], F32, name="half_rows")
-        weights = held.tile([PARTS, CHILDREN, PARTS], BF16, name="weights")
-        a_in_a_row = a.rearrange("c j -> (c j)")
-        nc.sync.dma_start(half_rows[:], a_in_a_row[0 : PARTS * STRIDE].rearrange("(k e) -> k e", e=STRIDE)[:, 0:HALF_ROW])
-        nc.sync.dma_start(offsets[:], offs)
+        a_rows = held.tile([PARTS, PARENTS], F32, name="a_rows")
+        w_rows = held.tile([PARTS, W_ROWS, PARTS], BF16, name="w_rows")
+        for t in range(CHILDREN):
+            nc.sync.dma_start(a_rows[t * TYPES : (t + 1) * TYPES, :], a[0:PARTS:ROWS_PER_TYPE, t * PARENTS : (t + 1) * PARENTS])
         nc.sync.dma_start(x_blocks[0][:], x[0:PARTS, :])
-        nc.sync.dma_start(weights[:], w.rearrange("(t q) m -> q t m", q=PARTS))
+        nc.sync.dma_start(offsets[:], offs)
+        nc.sync.dma_start(w_rows[:], w.rearrange("(k r) m -> k r m", r=W_ROWS))
         for i in range(1, BLOCKS):
             nc.sync.dma_start(x_blocks[i][:], x[i * PARTS : (i + 1) * PARTS, :])
 
-        holds = held.tile([PARTS, HALVES, TYPES], F32, name="holds")
-        nc.gpsimd.memset(holds[:], 0.0)
-        for value in (0, 2, 4):
-            nc.gpsimd.affine_select(
-                holds[:],
-                holds[:],
-                pattern=[[-1, HALVES], [-8, TYPES]],
-                compare_op=mybir.AluOpType.not_equal,
-                fill=1.0,
-                base=-value,
-                channel_multiplier=3,
-            )
-        member = held.tile([PARTS, HALVES], F32, name="member")
-        nc.vector.reduce_sum(member[:], holds[:], axis=mybir.AxisListType.X)
-        members = held.tile([PARTS, HALVES, PARTS], BF16, name="members")
-        nc.vector.tensor_copy(members[:], member[:].unsqueeze(2).to_broadcast([PARTS, HALVES, PARTS]))
-        pick = held.tile([PARTS, HALVES, TYPES, ROWS_PER_TYPE], F32, name="pick")
-        nc.vector.tensor_copy(pick[:], holds[:].unsqueeze(3).to_broadcast([PARTS, HALVES, TYPES, ROWS_PER_TYPE]))
-
-        half_rows_rounded = held.tile([PARTS, HALF_ROW], BF16, name="half_rows_rounded")
-        nc.scalar.copy(half_rows_rounded[:], half_rows[:])
+        ones = held.tile([PARTS, PARTS], BF16, name="ones")
+        nc.vector.memset(ones[:], 1.0)
+        a_rounded = held.tile([PARTS, PARENTS], BF16, name="a_rounded")
+        nc.vector.tensor_copy(a_rounded[:], a_rows[:])
         den = den_bank.tile([PARTS, PARENTS], F32, name="den")
-        for t in range(CHILDREN):
-            h, child_of_half = divmod(t, HALF_CHILDREN)
-            nc.tensor.matmul(
-                den[:],
-                members[:, h, :],
-                half_rows_rounded[:, child_of_half * PARENTS : (child_of_half + 1) * PARENTS],
-                start=(t == 0),
-                stop=(t == CHILDREN - 1),
-            )
+        nc.tensor.matmul(den[:], ones[:], a_rounded[:])
         den_inverse = held.tile([PARTS, PARENTS], F32, name="den_inverse")
         nc.vector.reciprocal(den_inverse[:], den[:])
-        divided = held.tile([PARTS, HALF_CHILDREN, PARENTS], F32, name="divided")
-        nc.vector.tensor_tensor(
-            divided[:],
-            half_rows[:].rearrange("k (t p) -> k t p", t=HALF_CHILDREN),
-            den_inverse[:].unsqueeze(1).to_broadcast([PARTS, HALF_CHILDREN, PARENTS]),
-            MULT,
-        )
+        rows_divided = held.tile([PARTS, PARENTS], F32, name="rows_divided")
+        nc.vector.tensor_tensor(rows_divided[:], a_rows[:], den_inverse[:], MULT)
 
+        identity = held.tile([PARTS, PARTS], F32, name="identity")
+        make_identity(nc, identity[:])
+        pick = held.tile([PARTS, PARTS, ROWS_PER_TYPE], F32, name="pick")
+        nc.scalar.copy(pick[:], identity[:].unsqueeze(2).to_broadcast([PARTS, PARTS, ROWS_PER_TYPE]))
+        pick = pick[:].rearrange("k j r -> k (j r)")
         a_divided = held.tile([PARTS, ENTRIES], F32, name="a_divided")
-        for h in range(HALVES):
-            spread = a_banks.tile([PARTS, HALF_ROW], F32, name=f"spread{h}")
-            for child_of_half in range(HALF_CHILDREN):
-                columns = slice(child_of_half * PARENTS, (child_of_half + 1) * PARENTS)
-                first_entry = (h * HALF_CHILDREN + child_of_half) * PARENTS
-                nc.tensor.matmul(spread[:, columns], pick[:, h, :, :].rearrange("k u r -> k (u r)"), divided[:, child_of_half, :])
-                nc.scalar.copy(a_divided[:, first_entry : first_entry + PARENTS], spread[:, columns])
+        for t in range(CHILDREN):
+            pair, half_of_bank = divmod(t, BANK // PARENTS)
+            if half_of_bank == 0:
+                spread = a_banks.tile([PARTS, BANK], F32, name=f"spread{pair}")
+            columns = slice(half_of_bank * PARENTS, (half_of_bank + 1) * PARENTS)
+            nc.tensor.matmul(spread[:, columns], pick[:, t * PARTS : (t + 1) * PARTS], rows_divided[:])
+            nc.scalar.copy(a_divided[:, t * PARENTS : (t + 1) * PARENTS], spread[:, columns])
+
+        band = held.tile([PARTS, BAND], BF16, name="band")
+        nc.gpsimd.memset(band[:], 1.0)
+        nc.gpsimd.affine_select(
+            band[:],
+            band[:],
+            pattern=[[-1, BAND]],
+            compare_op=mybir.AluOpType.is_equal,
+            fill=0.0,
+            base=W_ROWS - 1,
+            channel_multiplier=W_ROWS,
+        )
+        w_moved = w_bank.tile([PARTS, CHILDREN, PARTS], F32, name="w_moved")
+        for t in range(CHILDREN):
+            for r in range(W_ROWS):
+                first = t * PARTS - r + W_ROWS - 1
+                nc.tensor.matmul(w_moved[:, t, :], band[:, first : first + PARTS], w_rows[:, r, :], start=(r == 0), stop=(r == W_ROWS - 1))
+        weights = held.tile([PARTS, CHILDREN, PARTS], BF16, name="weights")
+        nc.scalar.copy(weights[:], w_moved[:])
 
         def look_up(i, first_entry, count, rounder):
             piece_offsets = offsets[:, first_entry // PER_COLUMN : (first_entry + count) // PER_COLUMN]

@@ -40,39 +40,38 @@ def tile_convcaps_kernel(tc, x, a, w, offs, out):
     ):
         x_blocks = [held.tile([PARTS, PLACES], F32, name=f"x_block{i}") for i in range(BLOCKS)]
         offsets = held.tile([PARTS, ENTRIES // PER_COLUMN], U16, name="offsets")
-        a_rows = held.tile([PARTS, PARENTS], F32, name="a_rows")
+        a_rows = held.tile([TYPES, CHILDREN, PARENTS], F32, name="a_rows")
         w_rows = held.tile([PARTS, W_ROWS, PARTS], BF16, name="w_rows")
-        for t in range(CHILDREN):
-            nc.sync.dma_start(a_rows[t * TYPES : (t + 1) * TYPES, :], a[0:PARTS:ROWS_PER_TYPE, t * PARENTS : (t + 1) * PARENTS])
+        nc.sync.dma_start(a_rows[:], a[0:PARTS:ROWS_PER_TYPE, :].rearrange("u (t p) -> u t p", t=CHILDREN))
         nc.sync.dma_start(x_blocks[0][:], x[0:PARTS, :])
         nc.sync.dma_start(offsets[:], offs)
         nc.sync.dma_start(w_rows[:], w.rearrange("(k r) m -> k r m", r=W_ROWS))
         for i in range(1, BLOCKS):
             nc.sync.dma_start(x_blocks[i][:], x[i * PARTS : (i + 1) * PARTS, :])
 
-        ones = held.tile([PARTS, PARTS], BF16, name="ones")
+        ones = held.tile([TYPES, PARTS], BF16, name="ones")
         nc.vector.memset(ones[:], 1.0)
-        a_rounded = held.tile([PARTS, PARENTS], BF16, name="a_rounded")
+        a_rounded = held.tile([TYPES, CHILDREN, PARENTS], BF16, name="a_rounded")
         nc.vector.tensor_copy(a_rounded[:], a_rows[:])
         den = den_bank.tile([PARTS, PARENTS], F32, name="den")
-        nc.tensor.matmul(den[:], ones[:], a_rounded[:])
-        den_inverse = held.tile([PARTS, PARENTS], F32, name="den_inverse")
-        nc.vector.reciprocal(den_inverse[:], den[:])
-        rows_divided = held.tile([PARTS, PARENTS], F32, name="rows_divided")
-        nc.vector.tensor_tensor(rows_divided[:], a_rows[:], den_inverse[:], MULT)
+        for t in range(CHILDREN):
+            nc.tensor.matmul(den[:], ones[:], a_rounded[:, t, :], start=(t == 0), stop=(t == CHILDREN - 1))
+        den_inverse = held.tile([TYPES, PARENTS], F32, name="den_inverse")
+        nc.vector.reciprocal(den_inverse[:], den[0:TYPES, :])
 
-        identity = held.tile([PARTS, PARTS], F32, name="identity")
+        identity = held.tile([TYPES, TYPES], F32, name="identity")
         make_identity(nc, identity[:])
-        pick = held.tile([PARTS, PARTS, ROWS_PER_TYPE], F32, name="pick")
-        nc.scalar.copy(pick[:], identity[:].unsqueeze(2).to_broadcast([PARTS, PARTS, ROWS_PER_TYPE]))
-        pick = pick[:].rearrange("k j r -> k (j r)")
+        pick = held.tile([TYPES, TYPES, ROWS_PER_TYPE], F32, name="pick")
+        nc.scalar.copy(pick[:], identity[:].unsqueeze(2).to_broadcast([TYPES, TYPES, ROWS_PER_TYPE]))
+        rows_divided = held.tile([TYPES, CHILDREN, PARENTS], F32, name="rows_divided")
         a_divided = held.tile([PARTS, ENTRIES], F32, name="a_divided")
         for t in range(CHILDREN):
+            nc.vector.tensor_tensor(rows_divided[:, t, :], a_rows[:, t, :], den_inverse[:], MULT)
             pair, half_of_bank = divmod(t, BANK // PARENTS)
             if half_of_bank == 0:
                 spread = a_banks.tile([PARTS, BANK], F32, name=f"spread{pair}")
             columns = slice(half_of_bank * PARENTS, (half_of_bank + 1) * PARENTS)
-            nc.tensor.matmul(spread[:, columns], pick[:, t * PARTS : (t + 1) * PARTS], rows_divided[:])
+            nc.tensor.matmul(spread[:, columns], pick[:].rearrange("k j r -> k (j r)"), rows_divided[:, t, :])
             nc.scalar.copy(a_divided[:, t * PARENTS : (t + 1) * PARENTS], spread[:, columns])
 
         band = held.tile([PARTS, BAND], BF16, name="band")

import concourse.mybir as mybir
from concourse.masks import make_identity

F32 = mybir.dt.float32
BF16 = mybir.dt.bfloat16
U16 = mybir.dt.uint16
MULT = mybir.AluOpType.mult

PARTS = 128
BLOCKS = 4
PLACES = 4096
CHILDREN = 4
PARENTS = 256
ENTRIES = CHILDREN * PARENTS
PER_COLUMN = 16
HALF = PARENTS // 2
LONGEST = ENTRIES // 2
BANK = 512

TYPES = 32
ROWS_PER_TYPE = PARTS // TYPES
W_ROWS = CHILDREN
BAND = (CHILDREN - 1) * PARTS + W_ROWS - 1 + PARTS

FLOPS = 2 * BLOCKS * CHILDREN * PARTS * PARTS * PARENTS
BYTES = 4 * BLOCKS * PARTS * PLACES + 4 * TYPES * ENTRIES + 2 * CHILDREN * PARTS * PARTS + 2 * PARTS * ENTRIES // PER_COLUMN + 4 * BLOCKS * PARTS * PARENTS


def tile_convcaps_kernel(tc, x, a, w, offs, out):
    nc = tc.nc
    with (
        tc.tile_pool(name="held", bufs=1) as held,
        tc.tile_pool(name="ring", bufs=4) as ring,
        tc.tile_pool(name="means", bufs=BLOCKS + 1) as means,
        tc.psum_pool(name="den_bank", bufs=1) as den_bank,
        tc.psum_pool(name="a_banks", bufs=1) as a_banks,
        tc.psum_pool(name="w_bank", bufs=1) as w_bank,
        tc.psum_pool(name="num_banks", bufs=2) as num_banks,
        tc.psum_pool(name="half_banks", bufs=1) as half_banks,
    ):
        x_blocks = [held.tile([PARTS, PLACES], F32, name=f"x_block{i}") for i in range(BLOCKS)]
        offsets = held.tile([PARTS, ENTRIES // PER_COLUMN], U16, name="offsets")
        a_rows = held.tile([TYPES, CHILDREN, PARENTS], F32, name="a_rows")
        w_rows = held.tile([PARTS, W_ROWS, PARTS], BF16, name="w_rows")
        nc.sync.dma_start(a_rows[:], a[0:PARTS:ROWS_PER_TYPE, :].rearrange("u (t p) -> u t p", t=CHILDREN))
        nc.sync.dma_start(x_blocks[0][:], x[0:PARTS, :])
        nc.sync.dma_start(offsets[:], offs)
        nc.sync.dma_start(w_rows[:], w.rearrange("(k r) m -> k r m", r=W_ROWS))
        for i in range(1, BLOCKS):
            nc.sync.dma_start(x_blocks[i][:], x[i * PARTS : (i + 1) * PARTS, :])

        ones = held.tile([TYPES, PARTS], BF16, name="ones")
        nc.vector.memset(ones[:], 1.0)
        a_rounded = held.tile([TYPES, CHILDREN, PARENTS], BF16, name="a_rounded")
        nc.vector.tensor_copy(a_rounded[:], a_rows[:])
        den = den_bank.tile([PARTS, PARENTS], F32, name="den")
        for t in range(CHILDREN):
            nc.tensor.matmul(den[:], ones[:], a_rounded[:, t, :], start=(t == 0), stop=(t == CHILDREN - 1))
        den_inverse = held.tile([TYPES, PARENTS], F32, name="den_inverse")
        nc.vector.reciprocal(den_inverse[:], den[0:TYPES, :])

        identity = held.tile([TYPES, TYPES], F32, name="identity")
        make_identity(nc, identity[:])
        pick = held.tile([TYPES, TYPES, ROWS_PER_TYPE], F32, name="pick")
        nc.scalar.copy(pick[:], identity[:].unsqueeze(2).to_broadcast([TYPES, TYPES, ROWS_PER_TYPE]))
        rows_divided = held.tile([TYPES, CHILDREN, PARENTS], F32, name="rows_divided")
        a_divided = held.tile([PARTS, ENTRIES], F32, name="a_divided")
        for t in range(CHILDREN):
            nc.vector.tensor_tensor(rows_divided[:, t, :], a_rows[:, t, :], den_inverse[:], MULT)
            pair, half_of_bank = divmod(t, BANK // PARENTS)
            if half_of_bank == 0:
                spread = a_banks.tile([PARTS, BANK], F32, name=f"spread{pair}")
            columns = slice(half_of_bank * PARENTS, (half_of_bank + 1) * PARENTS)
            nc.tensor.matmul(spread[:, columns], pick[:].rearrange("k j r -> k (j r)"), rows_divided[:, t, :])
            nc.scalar.copy(a_divided[:, t * PARENTS : (t + 1) * PARENTS], spread[:, columns])

        band = held.tile([PARTS, BAND], BF16, name="band")
        nc.gpsimd.memset(band[:], 1.0)
        nc.gpsimd.affine_select(
            band[:],
            band[:],
            pattern=[[-1, BAND]],
            compare_op=mybir.AluOpType.is_equal,
            fill=0.0,
            base=W_ROWS - 1,
            channel_multiplier=W_ROWS,
        )
        w_moved = w_bank.tile([PARTS, CHILDREN, PARTS], F32, name="w_moved")
        for t in range(CHILDREN):
            for r in range(W_ROWS):
                first = t * PARTS - r + W_ROWS - 1
                nc.tensor.matmul(w_moved[:, t, :], band[:, first : first + PARTS], w_rows[:, r, :], start=(r == 0), stop=(r == W_ROWS - 1))
        weights = held.tile([PARTS, CHILDREN, PARTS], BF16, name="weights")
        nc.scalar.copy(weights[:], w_moved[:])

        def look_up(i, first_entry, count, rounder):
            piece_offsets = offsets[:, first_entry // PER_COLUMN : (first_entry + count) // PER_COLUMN]
            z = ring.tile([PARTS, LONGEST], F32, name="z")
            nc.vector.tensor_tensor(
                z[:, :count], x_blocks[i][:].indirect(piece_offsets), a_divided[:, first_entry : first_entry + count], MULT
            )
            z_rounded = ring.tile([PARTS, LONGEST], BF16, name="z_rounded")
            for column in range(0, count, PARENTS):
                columns = slice(column, min(column + PARENTS, count))
                rounder(z_rounded[:, columns], z[:, columns])
            return z_rounded

        def copy_out_and_store(i, sums, first_parent, count):
            mean = means.tile([PARTS, PARENTS], F32, name="mean")
            nc.scalar.copy(mean[:, :count], sums)
            nc.sync.dma_start(out[i * PARTS : (i + 1) * PARTS, first_parent : first_parent + count], mean[:, :count])

        for i in range(BLOCKS - 1):
            num = num_banks.tile([PARTS, PARENTS], F32, name="num")
            for t in range(CHILDREN):
                z_rounded = look_up(i, t * PARENTS, PARENTS, nc.scalar.copy)
                nc.tensor.matmul(num[:], weights[:, t, :], z_rounded[:, :PARENTS], start=(t == 0), stop=(t == CHILDREN - 1))
            copy_out_and_store(i, num[:], 0, PARENTS)

        i = BLOCKS - 1
        pieces = []
        first_entry = 0
        while first_entry < ENTRIES:
            count = max((ENTRIES - first_entry) // 2, HALF)
            pieces.append((first_entry, count))
            first_entry += count
        half_nums = {first_parent: half_banks.tile([PARTS, BANK], F32, name=f"half_num{first_parent}") for first_parent in range(0, PARENTS, HALF)}
        for first_entry, count in pieces:
            last_piece = first_entry + count == ENTRIES
            z_rounded = look_up(i, first_entry, count, nc.vector.tensor_copy if last_piece else nc.scalar.copy)
            for column in range(0, count, HALF):
                t, first_parent = divmod(first_entry + column, PARENTS)
                nc.tensor.matmul(
                    half_nums[first_parent][:, :HALF],
                    weights[:, t, :],
                    z_rounded[:, column : column + HALF],
                    start=(t == 0),
                    stop=(t == CHILDREN - 1),
                )
        for first_parent in half_nums:
            copy_out_and_store(i, half_nums[first_parent][:, :HALF], first_parent, HALF)
